import numpy as np
import ml_dtypes


def mxq(x, axis, fmt="e4m3"):
    dtype, down = {"e4m3": (ml_dtypes.float8_e4m3fn, 7), "e5m2": (ml_dtypes.float8_e5m2, 14)}[fmt]
    v = np.moveaxis(np.asarray(x, np.float32).astype(ml_dtypes.bfloat16).astype(np.float64), axis, -1)
    blocks = v.reshape(v.shape[:-1] + (-1, 32))
    amax = np.abs(blocks).max(-1, keepdims=True)
    byte = np.maximum(np.where(amax > 0, np.frexp(amax)[1] - 1 + 127, 0) - down, 1)
    scale = np.exp2(byte - 127.0)
    codes = (blocks / scale).astype(np.float32).astype(dtype).astype(np.float64)
    return np.moveaxis((codes * scale).reshape(v.shape), -1, axis)


WIDE = False


def mx_kscale(k):
    if not WIDE:
        return np.ones(k)
    levels = np.array([10, -10, 5, -5, 0])
    a = np.random.permutation(np.resize(levels, k // 512 * 4)).reshape(k // 512, 4)
    idx = np.arange(k)
    return np.exp2(a[idx // 512, idx % 128 // 32])


BF16 = ml_dtypes.bfloat16


def bf(x):
    return np.asarray(x, np.float32).astype(BF16)


def f64(x):
    return np.asarray(x).astype(np.float64)


E2M1 = np.array([0.0, 0.5, 1.0, 1.5, 2.0, 3.0, 4.0, 6.0, -0.0, -0.5, -1.0, -1.5, -2.0, -3.0, -4.0, -6.0])


def pack_weight(w, fmt):
    k, n = w.shape
    w = f64(bf(w)).reshape(k // 32, 32, n)
    amax = np.abs(w).max(1)
    if fmt == "e4m3":
        byte = np.frexp(amax)[1] - 1 + 127 - 7
    else:
        mant, ex = np.frexp(amax / 6.0)
        byte = np.where(mant > 0.5, ex, ex - 1) + 127
    byte = np.clip(np.where(amax > 0, byte, 1), 1, 254)
    scaled = (w * np.exp2(127.0 - byte)[:, None, :]).reshape(k, n).astype(np.float32)
    by_word = np.ascontiguousarray(scaled.reshape(k // 512, 128, 4, n).transpose(0, 1, 3, 2))
    if fmt == "e4m3":
        words = by_word.astype(ml_dtypes.float8_e4m3fn).view(np.uint8)
    else:
        c = by_word.astype(ml_dtypes.float4_e2m1fn).view(np.uint8) & 0xF
        words = c[..., 0::2] | (c[..., 1::2] << 4)
    return np.ascontiguousarray(words), np.ascontiguousarray(byte.astype(np.uint8).reshape(k // 512, 16, n))


def unpack_weight(words, scales, fmt):
    g, p, n, _ = words.shape
    if fmt == "e4m3":
        vals = np.ascontiguousarray(words).view(ml_dtypes.float8_e4m3fn).astype(np.float64)
    else:
        nib = np.empty((g, p, n, 4), np.uint8)
        nib[..., 0::2] = words & 0xF
        nib[..., 1::2] = words >> 4
        vals = E2M1[nib]
    vals = vals * np.repeat(np.exp2(scales.astype(np.float64) - 127.0), 8, axis=1)[..., None]
    return vals.transpose(0, 1, 3, 2).reshape(g * 512, n)


B, K, N = 128, 4096, 4096
EPS = 1e-5
GELU_C = 0.7978845608


def setup_inputs():
    s = mx_kscale(K)
    x = bf(np.random.standard_normal((B, K)) * s)
    words, scales = pack_weight(np.random.standard_normal((K, N)) * np.sqrt(2.0 / K) / s[:, None], "e4m3")
    return {"x": x,
            "weight_words": words,
            "weight_scales": scales,
            "bn_gamma": bf(np.random.uniform(0.5, 1.5, N)),
            "bn_beta": bf(np.random.standard_normal(N) * 0.1),
            "bn_mean": bf(np.random.standard_normal(N) * 0.1),
            "bn_var": bf(np.random.uniform(0.5, 1.5, N))}


def reference(x, weight_words, weight_scales, bn_gamma, bn_beta, bn_mean, bn_var):
    acc = mxq(f64(x), 1, "e4m3") @ unpack_weight(weight_words, weight_scales, "e4m3")
    x_norm = (acc - f64(bn_mean)) / np.sqrt(f64(bn_var) + EPS)
    bn_out = f64(bn_gamma) * x_norm + f64(bn_beta)
    gelu = 0.5 * bn_out * (1.0 + np.tanh(GELU_C * (bn_out + 0.044715 * bn_out * bn_out * bn_out)))
    return np.maximum(gelu, 0.0)

@@ -1,0 +1,168 @@
+from contextlib import ExitStack
+
+import concourse.mybir as mybir
+from concourse.masks import make_identity
+
+F32 = mybir.dt.float32
+BF16 = mybir.dt.bfloat16
+I32 = mybir.dt.int32
+U32 = mybir.dt.uint32
+U8 = mybir.dt.uint8
+FP8X4 = mybir.dt.float8_e4m3fn_x4
+ACT = mybir.ActivationFunctionType
+
+P = 128
+B, K, N = 128, 4096, 4096
+EPS = 1e-5
+PACK = 4
+K_PASS = P * PACK
+PASSES = K // K_PASS
+BANK = 512
+BLOCK = 1024
+BANKS_PER_BLOCK = BLOCK // BANK
+N_BLOCKS = N // BLOCK
+PLANES_PER_TILE = 4
+QUADRANT = 32
+VEC_ROWS = N // P
+
+FLOPS = 2 * B * K * N
+
+
+def tile_modelnew_w_kernel(
+    tc, x, weight_words, weight_scales, bn_gamma, bn_beta, bn_mean, bn_var, out
+):
+    nc = tc.nc
+    with ExitStack() as ctx:
+        ctx.enter_context(tc.manual_schedule())
+        keep = ctx.enter_context(tc.tile_pool(name="keep", bufs=1))
+        weights = ctx.enter_context(tc.tile_pool(name="weights", bufs=N_BLOCKS * PASSES))
+        results = ctx.enter_context(tc.tile_pool(name="results", bufs=N // BANK))
+        prep_psum = ctx.enter_context(tc.psum_pool(name="prep_psum", bufs=4))
+        acc_psum = ctx.enter_context(tc.psum_pool(name="acc_psum", bufs=2 * BANKS_PER_BLOCK))
+
+        x_sb = keep.tile([P, K], BF16)
+        nc.sync.dma_start(out=x_sb[:], in_=x)
+
+        bn_rows = keep.tile([P, P], BF16)
+        for a, vec in enumerate((bn_gamma, bn_beta, bn_mean, bn_var)):
+            nc.scalar.dma_start(
+                out=bn_rows[VEC_ROWS * a : VEC_ROWS * (a + 1), :],
+                in_=vec.rearrange("(m p) -> m p", p=P),
+            )
+
+        w_planes = []
+        for h in range(PASSES // PLANES_PER_TILE):
+            planes = keep.tile([P, N], U8, name="planes%d" % h, align_bytes=64)
+            nc.vector.memset(planes[:].bitcast(I32), 0)
+            for quad in range(P // QUADRANT):
+                nc.sync.dma_start(
+                    out=planes[QUADRANT * quad : QUADRANT * quad + 4 * PLANES_PER_TILE, :].bitcast(I32),
+                    in_=weight_scales[
+                        PLANES_PER_TILE * h : PLANES_PER_TILE * (h + 1), 4 * quad : 4 * quad + 4, :
+                    ].bitcast(I32),
+                )
+            w_planes.append(planes)
+
+        words_dram = weight_words.rearrange("g p n t -> g p (n t)")
+        w_words = {}
+        for blk in range(N_BLOCKS):
+            for g in range(PASSES):
+                w = weights.tile([P, BLOCK], U32, align_bytes=64)
+                nc.sync.dma_start(
+                    out=w[:].bitcast(I32),
+                    in_=words_dram[g, :, PACK * BLOCK * blk : PACK * BLOCK * (blk + 1)].bitcast(I32),
+                )
+                w_words[(blk, g)] = w
+
+        ident = keep.tile([P, P], F32)
+        make_identity(nc, ident[:])
+
+        bn_rows_f32 = keep.tile([P, P], F32)
+        nc.vector.tensor_copy(out=bn_rows_f32[:], in_=bn_rows[:])
+        bn_t = prep_psum.tile([P, P], F32, tag="prep")
+        nc.tensor.transpose(bn_t[:], bn_rows_f32[:], ident[:])
+        bn_cols = keep.tile([P, 4, VEC_ROWS], F32)
+        nc.vector.tensor_copy(out=bn_cols[:].rearrange("p a m -> p (a m)"), in_=bn_t[:])
+        gamma = bn_cols[:, 0, :]
+        beta = bn_cols[:, 1, :]
+        mean = bn_cols[:, 2, :]
+        var = bn_cols[:, 3, :]
+        std = keep.tile([P, VEC_ROWS], F32)
+        nc.vector.tensor_scalar_add(out=std[:], in0=var, scalar1=EPS)
+        nc.scalar.sqrt(out=std[:], in_=std[:])
+
+        x_pairs = x_sb[:].bitcast(F32)
+        x_grouped = keep.tile([P, PASSES, B, PACK], BF16, align_bytes=64)
+        x_grouped_pairs = x_grouped[:].bitcast(F32)
+        for c in range(PASSES // 2):
+            xt = prep_psum.tile([P, 2, 2, B], F32, tag="prep")
+            for i in range(2):
+                g = 2 * c + i
+                for u in range(2):
+                    nc.tensor.transpose(
+                        xt[:, i, u, :], x_pairs[:, 256 * g + u : 256 * (g + 1) : 2], ident[:]
+                    )
+            copy = nc.vector.tensor_copy if c % 2 == 0 else nc.scalar.copy
+            copy(
+                out=x_grouped_pairs[:, 2 * c : 2 * c + 2, :, :],
+                in_=xt[:].rearrange("p i u b -> p i b u"),
+            )
+        x_codes = keep.tile([P, PASSES, B], U32, align_bytes=64)
+        x_scales = keep.tile([P, PASSES, B], U8, align_bytes=64)
+        nc.vector.quantize_mx(
+            out=x_codes[:].rearrange("p g b -> p (g b)").bitcast(FP8X4),
+            scales=x_scales[:].rearrange("p g b -> p (g b)"),
+            in_=x_grouped[:].rearrange("p g b t -> p (g b t)"),
+        )
+
+        gain = keep.tile([P, VEC_ROWS], F32)
+        shift = keep.tile([P, VEC_ROWS], F32)
+        nc.vector.reciprocal(out=gain[:], in_=std[:])
+        nc.vector.tensor_mul(out=gain[:], in0=gain[:], in1=gamma)
+        nc.vector.tensor_mul(out=shift[:], in0=mean, in1=gain[:])
+        nc.vector.tensor_sub(out=shift[:], in0=beta, in1=shift[:])
+
+        gain_all = keep.tile([P, N], F32)
+        shift_all = keep.tile([P, N], F32)
+        for c in range(N // BANK):
+            cols = slice(BANK * c, BANK * (c + 1))
+            for column, spread, copy in (
+                (gain, gain_all, nc.vector.tensor_copy),
+                (shift, shift_all, nc.scalar.copy),
+            ):
+                rows = prep_psum.tile([P, BANK], F32, tag="prep")
+                for i in range(BANK // P):
+                    m = (BANK // P) * c + i
+                    nc.tensor.transpose(
+                        rows[:, P * i : P * (i + 1)],
+                        column[:, m : m + 1].to_broadcast([P, P]),
+                        ident[:],
+                    )
+                copy(out=spread[:, cols], in_=rows[:])
+
+        for blk in range(N_BLOCKS):
+            accs = []
+            for j in range(BANKS_PER_BLOCK):
+                acc = acc_psum.tile([P, BANK], F32)
+                accs.append(acc)
+            for g in range(PASSES):
+                offset = 4 * (g % PLANES_PER_TILE)
+                for j in range(BANKS_PER_BLOCK):
+                    first = BLOCK * blk + BANK * j
+                    nc.tensor.matmul_mx(
+                        out=accs[j][:],
+                        lhsT=x_codes[:, g, :].bitcast(FP8X4),
+                        lhsT_scale=x_scales[:, g, :],
+                        rhs=w_words[(blk, g)][:, BANK * j : BANK * (j + 1)].bitcast(FP8X4),
+                        rhs_scale=w_planes[g // PLANES_PER_TILE][offset:P, first : first + BANK],
+                        start=(g == 0),
+                        stop=(g == PASSES - 1),
+                    )
+            for j in range(BANKS_PER_BLOCK):
+                cols = slice(BLOCK * blk + BANK * j, BLOCK * blk + BANK * (j + 1))
+                y = results.tile([P, BANK], F32)
+                nc.vector.tensor_mul(out=y[:], in0=accs[j][:], in1=gain_all[:, cols])
+                nc.vector.tensor_add(out=y[:], in0=y[:], in1=shift_all[:, cols])
+                nc.vector.tensor_scalar_max(out=y[:], in0=y[:], scalar1=0.0)
+                nc.scalar.activation(out=y[:], in_=y[:], func=ACT.Gelu_apprx_tanh)
+                nc.sync.dma_start(out=out[:, cols], in_=y[:])

@@ -40,6 +40,9 @@ def tile_modelnew_w_kernel(
         prep_psum = ctx.enter_context(tc.psum_pool(name="prep_psum", bufs=4))
         acc_psum = ctx.enter_context(tc.psum_pool(name="acc_psum", bufs=2 * BANKS_PER_BLOCK))
 
+        ident = keep.tile([P, P], F32)
+        make_identity(nc, ident[:])
+
         x_sb = keep.tile([P, K], BF16)
         nc.sync.dma_start(out=x_sb[:], in_=x)
 
@@ -55,11 +58,11 @@ def tile_modelnew_w_kernel(
             planes = keep.tile([P, N], U8, name="planes%d" % h, align_bytes=64)
             nc.vector.memset(planes[:].bitcast(I32), 0)
             for quad in range(P // QUADRANT):
-                nc.sync.dma_start(
-                    out=planes[QUADRANT * quad : QUADRANT * quad + 4 * PLANES_PER_TILE, :].bitcast(I32),
+                nc.gpsimd.dma_start(
+                    out=planes[QUADRANT * quad : QUADRANT * quad + 4 * PLANES_PER_TILE, :].bitcast(F32),
                     in_=weight_scales[
                         PLANES_PER_TILE * h : PLANES_PER_TILE * (h + 1), 4 * quad : 4 * quad + 4, :
-                    ].bitcast(I32),
+                    ].bitcast(F32),
                 )
             w_planes.append(planes)
 
@@ -73,9 +76,6 @@ def tile_modelnew_w_kernel(
                     in_=words_dram[g, :, PACK * BLOCK * blk : PACK * BLOCK * (blk + 1)].bitcast(I32),
                 )
                 w_words[(blk, g)] = w
-
-        ident = keep.tile([P, P], F32)
-        make_identity(nc, ident[:])
 
         bn_rows_f32 = keep.tile([P, P], F32)
         nc.vector.tensor_copy(out=bn_rows_f32[:], in_=bn_rows[:])

@@ -18,9 +18,10 @@ PACK = 4
 K_PASS = P * PACK
 PASSES = K // K_PASS
 BANK = 512
+N_BANKS = N // BANK
+WIDE_PASSES = 4
 BLOCK = 1024
-BANKS_PER_BLOCK = BLOCK // BANK
-N_BLOCKS = N // BLOCK
+BLOCK_WIDTHS = [BLOCK] * (N // BLOCK - 1) + [BLOCK // 2] * 2
 PLANES_PER_TILE = 4
 QUADRANT = 32
 VEC_ROWS = N // P
@@ -35,10 +36,11 @@ def tile_modelnew_w_kernel(
     with ExitStack() as ctx:
         ctx.enter_context(tc.manual_schedule())
         keep = ctx.enter_context(tc.tile_pool(name="keep", bufs=1))
-        weights = ctx.enter_context(tc.tile_pool(name="weights", bufs=N_BLOCKS * PASSES))
-        results = ctx.enter_context(tc.tile_pool(name="results", bufs=N // BANK))
-        prep_psum = ctx.enter_context(tc.psum_pool(name="prep_psum", bufs=4))
-        acc_psum = ctx.enter_context(tc.psum_pool(name="acc_psum", bufs=2 * BANKS_PER_BLOCK))
+        wide_pool = ctx.enter_context(tc.tile_pool(name="wide", bufs=WIDE_PASSES))
+        block_pool = ctx.enter_context(
+            tc.tile_pool(name="block", bufs=len(BLOCK_WIDTHS) * (PASSES - WIDE_PASSES))
+        )
+        results = ctx.enter_context(tc.tile_pool(name="results", bufs=len(BLOCK_WIDTHS)))
 
         ident = keep.tile([P, P], F32)
         make_identity(nc, ident[:])
@@ -58,111 +60,147 @@ def tile_modelnew_w_kernel(
             planes = keep.tile([P, N], U8, name="planes%d" % h, align_bytes=64)
             nc.vector.memset(planes[:].bitcast(I32), 0)
             for quad in range(P // QUADRANT):
-                nc.gpsimd.dma_start(
-                    out=planes[QUADRANT * quad : QUADRANT * quad + 4 * PLANES_PER_TILE, :].bitcast(F32),
+                nc.sync.dma_start(
+                    out=planes[QUADRANT * quad : QUADRANT * quad + 4 * PLANES_PER_TILE, :].bitcast(I32),
                     in_=weight_scales[
                         PLANES_PER_TILE * h : PLANES_PER_TILE * (h + 1), 4 * quad : 4 * quad + 4, :
-                    ].bitcast(F32),
+                    ].bitcast(I32),
                 )
             w_planes.append(planes)
 
         words_dram = weight_words.rearrange("g p n t -> g p (n t)")
         w_words = {}
-        for blk in range(N_BLOCKS):
-            for g in range(PASSES):
-                w = weights.tile([P, BLOCK], U32, align_bytes=64)
+        for g in range(WIDE_PASSES):
+            wide = wide_pool.tile([P, N], U32, align_bytes=64)
+            nc.sync.dma_start(out=wide[:].bitcast(I32), in_=words_dram[g].bitcast(I32))
+            for bank in range(N_BANKS):
+                w_words[(g, bank)] = wide[:, BANK * bank : BANK * (bank + 1)]
+        first = 0
+        for width in BLOCK_WIDTHS:
+            for g in range(WIDE_PASSES, PASSES):
+                part = block_pool.tile([P, width], U32, align_bytes=64)
                 nc.sync.dma_start(
-                    out=w[:].bitcast(I32),
-                    in_=words_dram[g, :, PACK * BLOCK * blk : PACK * BLOCK * (blk + 1)].bitcast(I32),
+                    out=part[:].bitcast(I32),
+                    in_=words_dram[g, :, PACK * first : PACK * (first + width)].bitcast(I32),
                 )
-                w_words[(blk, g)] = w
-
-        bn_rows_f32 = keep.tile([P, P], F32)
-        nc.vector.tensor_copy(out=bn_rows_f32[:], in_=bn_rows[:])
-        bn_t = prep_psum.tile([P, P], F32, tag="prep")
-        nc.tensor.transpose(bn_t[:], bn_rows_f32[:], ident[:])
-        bn_cols = keep.tile([P, 4, VEC_ROWS], F32)
-        nc.vector.tensor_copy(out=bn_cols[:].rearrange("p a m -> p (a m)"), in_=bn_t[:])
-        gamma = bn_cols[:, 0, :]
-        beta = bn_cols[:, 1, :]
-        mean = bn_cols[:, 2, :]
-        var = bn_cols[:, 3, :]
-        std = keep.tile([P, VEC_ROWS], F32)
-        nc.vector.tensor_scalar_add(out=std[:], in0=var, scalar1=EPS)
-        nc.scalar.sqrt(out=std[:], in_=std[:])
-
-        x_pairs = x_sb[:].bitcast(F32)
-        x_grouped = keep.tile([P, PASSES, B, PACK], BF16, align_bytes=64)
-        x_grouped_pairs = x_grouped[:].bitcast(F32)
-        for c in range(PASSES // 2):
-            xt = prep_psum.tile([P, 2, 2, B], F32, tag="prep")
-            for i in range(2):
-                g = 2 * c + i
-                for u in range(2):
-                    nc.tensor.transpose(
-                        xt[:, i, u, :], x_pairs[:, 256 * g + u : 256 * (g + 1) : 2], ident[:]
-                    )
-            copy = nc.vector.tensor_copy if c % 2 == 0 else nc.scalar.copy
-            copy(
-                out=x_grouped_pairs[:, 2 * c : 2 * c + 2, :, :],
-                in_=xt[:].rearrange("p i u b -> p i b u"),
-            )
-        x_codes = keep.tile([P, PASSES, B], U32, align_bytes=64)
-        x_scales = keep.tile([P, PASSES, B], U8, align_bytes=64)
-        nc.vector.quantize_mx(
-            out=x_codes[:].rearrange("p g b -> p (g b)").bitcast(FP8X4),
-            scales=x_scales[:].rearrange("p g b -> p (g b)"),
-            in_=x_grouped[:].rearrange("p g b t -> p (g b t)"),
-        )
-
-        gain = keep.tile([P, VEC_ROWS], F32)
-        shift = keep.tile([P, VEC_ROWS], F32)
-        nc.vector.reciprocal(out=gain[:], in_=std[:])
-        nc.vector.tensor_mul(out=gain[:], in0=gain[:], in1=gamma)
-        nc.vector.tensor_mul(out=shift[:], in0=mean, in1=gain[:])
-        nc.vector.tensor_sub(out=shift[:], in0=beta, in1=shift[:])
+                for j in range(width // BANK):
+                    w_words[(g, first // BANK + j)] = part[:, BANK * j : BANK * (j + 1)]
+            first += width
 
         gain_all = keep.tile([P, N], F32)
         shift_all = keep.tile([P, N], F32)
-        for c in range(N // BANK):
-            cols = slice(BANK * c, BANK * (c + 1))
-            for column, spread, copy in (
-                (gain, gain_all, nc.vector.tensor_copy),
-                (shift, shift_all, nc.scalar.copy),
-            ):
-                rows = prep_psum.tile([P, BANK], F32, tag="prep")
-                for i in range(BANK // P):
-                    m = (BANK // P) * c + i
-                    nc.tensor.transpose(
-                        rows[:, P * i : P * (i + 1)],
-                        column[:, m : m + 1].to_broadcast([P, P]),
-                        ident[:],
-                    )
-                copy(out=spread[:, cols], in_=rows[:])
+        x_codes = keep.tile([P, PASSES, B], U32, align_bytes=64)
+        x_scales = keep.tile([P, PASSES, B], U8, align_bytes=64)
 
-        for blk in range(N_BLOCKS):
-            accs = []
-            for j in range(BANKS_PER_BLOCK):
-                acc = acc_psum.tile([P, BANK], F32)
-                accs.append(acc)
-            for g in range(PASSES):
-                offset = 4 * (g % PLANES_PER_TILE)
-                for j in range(BANKS_PER_BLOCK):
-                    first = BLOCK * blk + BANK * j
-                    nc.tensor.matmul_mx(
-                        out=accs[j][:],
-                        lhsT=x_codes[:, g, :].bitcast(FP8X4),
-                        lhsT_scale=x_scales[:, g, :],
-                        rhs=w_words[(blk, g)][:, BANK * j : BANK * (j + 1)].bitcast(FP8X4),
-                        rhs_scale=w_planes[g // PLANES_PER_TILE][offset:P, first : first + BANK],
-                        start=(g == 0),
-                        stop=(g == PASSES - 1),
-                    )
-            for j in range(BANKS_PER_BLOCK):
-                cols = slice(BLOCK * blk + BANK * j, BLOCK * blk + BANK * (j + 1))
-                y = results.tile([P, BANK], F32)
-                nc.vector.tensor_mul(out=y[:], in0=accs[j][:], in1=gain_all[:, cols])
-                nc.vector.tensor_add(out=y[:], in0=y[:], in1=shift_all[:, cols])
-                nc.vector.tensor_scalar_max(out=y[:], in0=y[:], scalar1=0.0)
-                nc.scalar.activation(out=y[:], in_=y[:], func=ACT.Gelu_apprx_tanh)
-                nc.sync.dma_start(out=out[:, cols], in_=y[:])
+        with tc.psum_pool(name="prep_psum", bufs=N_BANKS) as prep_psum:
+            bn_rows_f32 = keep.tile([P, P], F32)
+            nc.vector.tensor_copy(out=bn_rows_f32[:], in_=bn_rows[:])
+            bn_t = prep_psum.tile([P, P], F32, tag="prep")
+            nc.tensor.transpose(bn_t[:], bn_rows_f32[:], ident[:])
+            bn_cols = keep.tile([P, 4, VEC_ROWS], F32)
+            nc.vector.tensor_copy(out=bn_cols[:].rearrange("p a m -> p (a m)"), in_=bn_t[:])
+            gamma = bn_cols[:, 0, :]
+            beta = bn_cols[:, 1, :]
+            mean = bn_cols[:, 2, :]
+            var = bn_cols[:, 3, :]
+            std = keep.tile([P, VEC_ROWS], F32)
+            nc.vector.tensor_scalar_add(out=std[:], in0=var, scalar1=EPS)
+            nc.scalar.sqrt(out=std[:], in_=std[:])
+
+            x_pairs = x_sb[:].bitcast(F32)
+            x_grouped = keep.tile([P, PASSES, B, PACK], BF16, align_bytes=64)
+            x_grouped_pairs = x_grouped[:].bitcast(F32)
+            for c in range(PASSES // 2):
+                xt = prep_psum.tile([P, 2, 2, B], F32, tag="prep")
+                for i in range(2):
+                    g = 2 * c + i
+                    for u in range(2):
+                        nc.tensor.transpose(
+                            xt[:, i, u, :], x_pairs[:, 256 * g + u : 256 * (g + 1) : 2], ident[:]
+                        )
+                copy = nc.vector.tensor_copy if c % 2 == 0 else nc.scalar.copy
+                copy(
+                    out=x_grouped_pairs[:, 2 * c : 2 * c + 2, :, :],
+                    in_=xt[:].rearrange("p i u b -> p i b u"),
+                )
+            nc.vector.quantize_mx(
+                out=x_codes[:].rearrange("p g b -> p (g b)").bitcast(FP8X4),
+                scales=x_scales[:].rearrange("p g b -> p (g b)"),
+                in_=x_grouped[:].rearrange("p g b t -> p (g b t)"),
+            )
+
+            gain = keep.tile([P, VEC_ROWS], F32)
+            shift = keep.tile([P, VEC_ROWS], F32)
+            nc.vector.reciprocal(out=gain[:], in_=std[:])
+            nc.vector.tensor_mul(out=gain[:], in0=gain[:], in1=gamma)
+            nc.vector.tensor_mul(out=shift[:], in0=mean, in1=gain[:])
+            nc.vector.tensor_sub(out=shift[:], in0=beta, in1=shift[:])
+
+            for c in range(N_BANKS):
+                cols = slice(BANK * c, BANK * (c + 1))
+                for column, spread, copy in (
+                    (gain, gain_all, nc.vector.tensor_copy),
+                    (shift, shift_all, nc.scalar.copy),
+                ):
+                    rows = prep_psum.tile([P, BANK], F32, tag="prep")
+                    for i in range(BANK // P):
+                        m = (BANK // P) * c + i
+                        nc.tensor.transpose(
+                            rows[:, P * i : P * (i + 1)],
+                            column[:, m : m + 1].to_broadcast([P, P]),
+                            ident[:],
+                        )
+                    copy(out=spread[:, cols], in_=rows[:])
+
+        acc_psum = ctx.enter_context(tc.psum_pool(name="acc_psum", bufs=N_BANKS))
+        accs = []
+        for bank in range(N_BANKS):
+            acc = acc_psum.tile([P, BANK], F32)
+            accs.append(acc)
+
+        def mx_pass(g, bank):
+            offset = 4 * (g % PLANES_PER_TILE)
+            nc.tensor.matmul_mx(
+                out=accs[bank][:],
+                lhsT=x_codes[:, g, :].bitcast(FP8X4),
+                lhsT_scale=x_scales[:, g, :],
+                rhs=w_words[(g, bank)].bitcast(FP8X4),
+                rhs_scale=w_planes[g // PLANES_PER_TILE][offset:P, BANK * bank : BANK * (bank + 1)],
+                start=(g == 0),
+                stop=(g == PASSES - 1),
+            )
+
+        for g in range(WIDE_PASSES):
+            for bank in range(N_BANKS):
+                mx_pass(g, bank)
+
+        first = 0
+        for width in BLOCK_WIDTHS:
+            for g in range(WIDE_PASSES, PASSES):
+                for j in range(width // BANK):
+                    mx_pass(g, first // BANK + j)
+            y = results.tile([P, width], F32)
+            half = width // 2
+            for lo in (0, half):
+                col = first + lo
+                nc.vector.tensor_mul(
+                    out=y[:, lo : lo + half],
+                    in0=accs[col // BANK][:, col % BANK : col % BANK + half],
+                    in1=gain_all[:, col : col + half],
+                )
+            for lo in (0, half):
+                nc.vector.tensor_add(
+                    out=y[:, lo : lo + half],
+                    in0=y[:, lo : lo + half],
+                    in1=shift_all[:, first + lo : first + lo + half],
+                )
+            for lo in (0, half):
+                nc.vector.tensor_scalar_max(
+                    out=y[:, lo : lo + half], in0=y[:, lo : lo + half], scalar1=0.0
+                )
+            for lo in (0, half):
+                nc.scalar.activation(
+                    out=y[:, lo : lo + half], in_=y[:, lo : lo + half], func=ACT.Gelu_apprx_tanh
+                )
+            nc.sync.dma_start(out=out[:, first : first + width], in_=y[:])
+            first += width

@@ -34,7 +34,6 @@ def tile_modelnew_w_kernel(
 ):
     nc = tc.nc
     with ExitStack() as ctx:
-        ctx.enter_context(tc.manual_schedule())
         keep = ctx.enter_context(tc.tile_pool(name="keep", bufs=1))
         wide_pool = ctx.enter_context(tc.tile_pool(name="wide", bufs=WIDE_PASSES))
         block_pool = ctx.enter_context(

@@ -21,7 +21,14 @@ BANK = 512
 N_BANKS = N // BANK
 WIDE_PASSES = 4
 BLOCK = 1024
-BLOCK_WIDTHS = [BLOCK] * (N // BLOCK - 1) + [BLOCK // 2] * 2
+BLOCKS = [
+    (1536, [(4, 5), (5, 6), (6, 7), (7, 8)]),
+    (1024, [(4, 5), (5, 6), (6, 7), (7, 8)]),
+    (768, [(4, 5), (5, 6), (6, 7), (7, 8)]),
+    (512, [(4, 5), (5, 6), (6, 7), (7, 8)]),
+    (256, [(2, 3), (3, 4), (4, 5), (5, 6), (6, 7), (7, 8)]),
+]
+WIDE_RUNS = [(0, 1, 4096), (1, 2, 4096), (2, 3, 3840), (3, 4, 3840)]
 PLANES_PER_TILE = 4
 QUADRANT = 32
 VEC_ROWS = N // P
@@ -35,11 +42,18 @@ def tile_modelnew_w_kernel(
     nc = tc.nc
     with ExitStack() as ctx:
         keep = ctx.enter_context(tc.tile_pool(name="keep", bufs=1))
-        wide_pool = ctx.enter_context(tc.tile_pool(name="wide", bufs=WIDE_PASSES))
-        block_pool = ctx.enter_context(
-            tc.tile_pool(name="block", bufs=len(BLOCK_WIDTHS) * (PASSES - WIDE_PASSES))
-        )
-        results = ctx.enter_context(tc.tile_pool(name="results", bufs=len(BLOCK_WIDTHS)))
+
+        BLOCK_WIDTHS = [width for width, runs in BLOCKS]
+        units = []
+        blocks = []
+        first = 0
+        for width in BLOCK_WIDTHS:
+            members = []
+            for lo in range(0, width, BANK):
+                members.append(len(units))
+                units.append((first + lo, min(BANK, width - lo)))
+            blocks.append(members)
+            first += width
 
         ident = keep.tile([P, P], F32)
         make_identity(nc, ident[:])
@@ -69,21 +83,28 @@ def tile_modelnew_w_kernel(
 
         words_dram = weight_words.rearrange("g p n t -> g p (n t)")
         w_words = {}
-        for g in range(WIDE_PASSES):
-            wide = wide_pool.tile([P, N], U32, align_bytes=64)
-            nc.sync.dma_start(out=wide[:].bitcast(I32), in_=words_dram[g].bitcast(I32))
-            for bank in range(N_BANKS):
-                w_words[(g, bank)] = wide[:, BANK * bank : BANK * (bank + 1)]
+
+        def load_words(g_lo, g_hi, first, width, members):
+            part = keep.tile(
+                [P, g_hi - g_lo, width], U32, name="w%d_%d" % (g_lo, first), align_bytes=64
+            )
+            nc.sync.dma_start(
+                out=part[:].bitcast(I32),
+                in_=words_dram[g_lo:g_hi, :, PACK * first : PACK * (first + width)]
+                .bitcast(I32)
+                .rearrange("g p n -> p g n"),
+            )
+            for g in range(g_lo, g_hi):
+                for u in members:
+                    lo, wid = units[u]
+                    w_words[(g, u)] = part[:, g - g_lo, lo - first : lo - first + wid]
+
+        for g_lo, g_hi, width in WIDE_RUNS:
+            load_words(g_lo, g_hi, 0, width, [u for u in range(len(units)) if units[u][0] < width])
         first = 0
-        for width in BLOCK_WIDTHS:
-            for g in range(WIDE_PASSES, PASSES):
-                part = block_pool.tile([P, width], U32, align_bytes=64)
-                nc.sync.dma_start(
-                    out=part[:].bitcast(I32),
-                    in_=words_dram[g, :, PACK * first : PACK * (first + width)].bitcast(I32),
-                )
-                for j in range(width // BANK):
-                    w_words[(g, first // BANK + j)] = part[:, BANK * j : BANK * (j + 1)]
+        for b, (width, runs) in enumerate(BLOCKS):
+            for g_lo, g_hi in runs:
+                load_words(g_lo, g_hi, first, width, blocks[b])
             first += width
 
         gain_all = keep.tile([P, N], F32)
@@ -153,53 +174,71 @@ def tile_modelnew_w_kernel(
 
         acc_psum = ctx.enter_context(tc.psum_pool(name="acc_psum", bufs=N_BANKS))
         accs = []
-        for bank in range(N_BANKS):
+
+        def open_unit():
             acc = acc_psum.tile([P, BANK], F32)
             accs.append(acc)
 
-        def mx_pass(g, bank):
+        def mx_pass(g, u):
             offset = 4 * (g % PLANES_PER_TILE)
+            lo, wid = units[u]
             nc.tensor.matmul_mx(
-                out=accs[bank][:],
+                out=accs[u][:, 0:wid],
                 lhsT=x_codes[:, g, :].bitcast(FP8X4),
                 lhsT_scale=x_scales[:, g, :],
-                rhs=w_words[(g, bank)].bitcast(FP8X4),
-                rhs_scale=w_planes[g // PLANES_PER_TILE][offset:P, BANK * bank : BANK * (bank + 1)],
+                rhs=w_words[(g, u)].bitcast(FP8X4),
+                rhs_scale=w_planes[g // PLANES_PER_TILE][offset:P, lo : lo + wid],
                 start=(g == 0),
                 stop=(g == PASSES - 1),
             )
 
+        for u in range(N_BANKS):
+            open_unit()
+        late_from = {}
+        for b, (width, runs) in enumerate(BLOCKS):
+            for u in blocks[b]:
+                late_from[u] = runs[0][0]
         for g in range(WIDE_PASSES):
-            for bank in range(N_BANKS):
-                mx_pass(g, bank)
+            for u in range(N_BANKS):
+                if g < late_from[u]:
+                    mx_pass(g, u)
 
         first = 0
-        for width in BLOCK_WIDTHS:
-            for g in range(WIDE_PASSES, PASSES):
-                for j in range(width // BANK):
-                    mx_pass(g, first // BANK + j)
-            y = results.tile([P, width], F32)
-            half = width // 2
-            for lo in (0, half):
-                col = first + lo
+        for b, width in enumerate(BLOCK_WIDTHS):
+            for g in range(BLOCKS[b][1][0][0], PASSES):
+                for u in blocks[b]:
+                    mx_pass(g, u)
+            y = keep.tile([P, width], F32, name="y%d" % b)
+            pieces = []
+            for u in blocks[b]:
+                lo, wid = units[u]
+                cut = wid if len(blocks[b]) > 1 else wid // 2
+                for off in range(0, wid, cut):
+                    pieces.append((u, off, lo - first + off, cut))
+            for u, off, lo, cut in pieces:
                 nc.vector.tensor_mul(
-                    out=y[:, lo : lo + half],
-                    in0=accs[col // BANK][:, col % BANK : col % BANK + half],
-                    in1=gain_all[:, col : col + half],
+                    out=y[:, lo : lo + cut],
+                    in0=accs[u][:, off : off + cut],
+                    in1=gain_all[:, first + lo : first + lo + cut],
                 )
-            for lo in (0, half):
+            for u, off, lo, cut in pieces:
                 nc.vector.tensor_add(
-                    out=y[:, lo : lo + half],
-                    in0=y[:, lo : lo + half],
-                    in1=shift_all[:, first + lo : first + lo + half],
+                    out=y[:, lo : lo + cut],
+                    in0=y[:, lo : lo + cut],
+                    in1=shift_all[:, first + lo : first + lo + cut],
                 )
-            for lo in (0, half):
-                nc.vector.tensor_scalar_max(
-                    out=y[:, lo : lo + half], in0=y[:, lo : lo + half], scalar1=0.0
-                )
-            for lo in (0, half):
+            for u, off, lo, cut in pieces:
+                nc.vector.tensor_scalar_max(out=y[:, lo : lo + cut], in0=y[:, lo : lo + cut], scalar1=0.0)
+            for u, off, lo, cut in pieces:
                 nc.scalar.activation(
-                    out=y[:, lo : lo + half], in_=y[:, lo : lo + half], func=ACT.Gelu_apprx_tanh
+                    out=y[:, lo : lo + cut], in_=y[:, lo : lo + cut], func=ACT.Gelu_apprx_tanh
                 )
             nc.sync.dma_start(out=out[:, first : first + width], in_=y[:])
             first += width
+            if b == 0:
+                for u in range(N_BANKS, len(units)):
+                    open_unit()
+                for g in range(WIDE_PASSES):
+                    for u in range(N_BANKS, len(units)):
+                        if g < late_from[u]:
+                            mx_pass(g, u)

@@ -233,7 +233,8 @@ def tile_modelnew_w_kernel(
                 nc.scalar.activation(
                     out=y[:, lo : lo + cut], in_=y[:, lo : lo + cut], func=ACT.Gelu_apprx_tanh
                 )
-            nc.sync.dma_start(out=out[:, first : first + width], in_=y[:])
+            queue = nc.scalar if b >= len(BLOCK_WIDTHS) - 2 else nc.sync
+            queue.dma_start(out=out[:, first : first + width], in_=y[:])
             first += width
             if b == 0:
                 for u in range(N_BANKS, len(units)):

from contextlib import ExitStack

import concourse.mybir as mybir
from concourse.masks import make_identity

F32 = mybir.dt.float32
BF16 = mybir.dt.bfloat16
I32 = mybir.dt.int32
U32 = mybir.dt.uint32
U8 = mybir.dt.uint8
FP8X4 = mybir.dt.float8_e4m3fn_x4
ACT = mybir.ActivationFunctionType

P = 128
B, K, N = 128, 4096, 4096
EPS = 1e-5
PACK = 4
K_PASS = P * PACK
PASSES = K // K_PASS
BANK = 512
N_BANKS = N // BANK
WIDE_PASSES = 4
BLOCK = 1024
BLOCKS = [
    (1536, [(4, 5), (5, 6), (6, 7), (7, 8)]),
    (1024, [(4, 5), (5, 6), (6, 7), (7, 8)]),
    (768, [(4, 5), (5, 6), (6, 7), (7, 8)]),
    (512, [(4, 5), (5, 6), (6, 7), (7, 8)]),
    (256, [(2, 3), (3, 4), (4, 5), (5, 6), (6, 7), (7, 8)]),
]
WIDE_RUNS = [(0, 1, 4096), (1, 2, 4096), (2, 3, 3840), (3, 4, 3840)]
PLANES_PER_TILE = 4
QUADRANT = 32
VEC_ROWS = N // P

FLOPS = 2 * B * K * N


def tile_modelnew_w_kernel(
    tc, x, weight_words, weight_scales, bn_gamma, bn_beta, bn_mean, bn_var, out
):
    nc = tc.nc
    with ExitStack() as ctx:
        keep = ctx.enter_context(tc.tile_pool(name="keep", bufs=1))

        BLOCK_WIDTHS = [width for width, runs in BLOCKS]
        units = []
        blocks = []
        first = 0
        for width in BLOCK_WIDTHS:
            members = []
            for lo in range(0, width, BANK):
                members.append(len(units))
                units.append((first + lo, min(BANK, width - lo)))
            blocks.append(members)
            first += width

        ident = keep.tile([P, P], F32)
        make_identity(nc, ident[:])

        x_sb = keep.tile([P, K], BF16)
        nc.sync.dma_start(out=x_sb[:], in_=x)

        bn_rows = keep.tile([P, P], BF16)
        for a, vec in enumerate((bn_gamma, bn_beta, bn_mean, bn_var)):
            nc.scalar.dma_start(
                out=bn_rows[VEC_ROWS * a : VEC_ROWS * (a + 1), :],
                in_=vec.rearrange("(m p) -> m p", p=P),
            )

        w_planes = []
        for h in range(PASSES // PLANES_PER_TILE):
            planes = keep.tile([P, N], U8, name="planes%d" % h, align_bytes=64)
            nc.vector.memset(planes[:].bitcast(I32), 0)
            for quad in range(P // QUADRANT):
                nc.sync.dma_start(
                    out=planes[QUADRANT * quad : QUADRANT * quad + 4 * PLANES_PER_TILE, :].bitcast(I32),
                    in_=weight_scales[
                        PLANES_PER_TILE * h : PLANES_PER_TILE * (h + 1), 4 * quad : 4 * quad + 4, :
                    ].bitcast(I32),
                )
            w_planes.append(planes)

        words_dram = weight_words.rearrange("g p n t -> g p (n t)")
        w_words = {}

        def load_words(g_lo, g_hi, first, width, members):
            part = keep.tile(
                [P, g_hi - g_lo, width], U32, name="w%d_%d" % (g_lo, first), align_bytes=64
            )
            nc.sync.dma_start(
                out=part[:].bitcast(I32),
                in_=words_dram[g_lo:g_hi, :, PACK * first : PACK * (first + width)]
                .bitcast(I32)
                .rearrange("g p n -> p g n"),
            )
            for g in range(g_lo, g_hi):
                for u in members:
                    lo, wid = units[u]
                    w_words[(g, u)] = part[:, g - g_lo, lo - first : lo - first + wid]

        for g_lo, g_hi, width in WIDE_RUNS:
            load_words(g_lo, g_hi, 0, width, [u for u in range(len(units)) if units[u][0] < width])
        first = 0
        for b, (width, runs) in enumerate(BLOCKS):
            for g_lo, g_hi in runs:
                load_words(g_lo, g_hi, first, width, blocks[b])
            first += width

        gain_all = keep.tile([P, N], F32)
        shift_all = keep.tile([P, N], F32)
        x_codes = keep.tile([P, PASSES, B], U32, align_bytes=64)
        x_scales = keep.tile([P, PASSES, B], U8, align_bytes=64)

        with tc.psum_pool(name="prep_psum", bufs=N_BANKS) as prep_psum:
            bn_rows_f32 = keep.tile([P, P], F32)
            nc.vector.tensor_copy(out=bn_rows_f32[:], in_=bn_rows[:])
            bn_t = prep_psum.tile([P, P], F32, tag="prep")
            nc.tensor.transpose(bn_t[:], bn_rows_f32[:], ident[:])
            bn_cols = keep.tile([P, 4, VEC_ROWS], F32)
            nc.vector.tensor_copy(out=bn_cols[:].rearrange("p a m -> p (a m)"), in_=bn_t[:])
            gamma = bn_cols[:, 0, :]
            beta = bn_cols[:, 1, :]
            mean = bn_cols[:, 2, :]
            var = bn_cols[:, 3, :]
            std = keep.tile([P, VEC_ROWS], F32)
            nc.vector.tensor_scalar_add(out=std[:], in0=var, scalar1=EPS)
            nc.scalar.sqrt(out=std[:], in_=std[:])

            x_pairs = x_sb[:].bitcast(F32)
            x_grouped = keep.tile([P, PASSES, B, PACK], BF16, align_bytes=64)
            x_grouped_pairs = x_grouped[:].bitcast(F32)
            for c in range(PASSES // 2):
                xt = prep_psum.tile([P, 2, 2, B], F32, tag="prep")
                for i in range(2):
                    g = 2 * c + i
                    for u in range(2):
                        nc.tensor.transpose(
                            xt[:, i, u, :], x_pairs[:, 256 * g + u : 256 * (g + 1) : 2], ident[:]
                        )
                copy = nc.vector.tensor_copy if c % 2 == 0 else nc.scalar.copy
                copy(
                    out=x_grouped_pairs[:, 2 * c : 2 * c + 2, :, :],
                    in_=xt[:].rearrange("p i u b -> p i b u"),
                )
            nc.vector.quantize_mx(
                out=x_codes[:].rearrange("p g b -> p (g b)").bitcast(FP8X4),
                scales=x_scales[:].rearrange("p g b -> p (g b)"),
                in_=x_grouped[:].rearrange("p g b t -> p (g b t)"),
            )

            gain = keep.tile([P, VEC_ROWS], F32)
            shift = keep.tile([P, VEC_ROWS], F32)
            nc.vector.reciprocal(out=gain[:], in_=std[:])
            nc.vector.tensor_mul(out=gain[:], in0=gain[:], in1=gamma)
            nc.vector.tensor_mul(out=shift[:], in0=mean, in1=gain[:])
            nc.vector.tensor_sub(out=shift[:], in0=beta, in1=shift[:])

            for c in range(N_BANKS):
                cols = slice(BANK * c, BANK * (c + 1))
                for column, spread, copy in (
                    (gain, gain_all, nc.vector.tensor_copy),
                    (shift, shift_all, nc.scalar.copy),
                ):
                    rows = prep_psum.tile([P, BANK], F32, tag="prep")
                    for i in range(BANK // P):
                        m = (BANK // P) * c + i
                        nc.tensor.transpose(
                            rows[:, P * i : P * (i + 1)],
                            column[:, m : m + 1].to_broadcast([P, P]),
                            ident[:],
                        )
                    copy(out=spread[:, cols], in_=rows[:])

        acc_psum = ctx.enter_context(tc.psum_pool(name="acc_psum", bufs=N_BANKS))
        accs = []

        def open_unit():
            acc = acc_psum.tile([P, BANK], F32)
            accs.append(acc)

        def mx_pass(g, u):
            offset = 4 * (g % PLANES_PER_TILE)
            lo, wid = units[u]
            nc.tensor.matmul_mx(
                out=accs[u][:, 0:wid],
                lhsT=x_codes[:, g, :].bitcast(FP8X4),
                lhsT_scale=x_scales[:, g, :],
                rhs=w_words[(g, u)].bitcast(FP8X4),
                rhs_scale=w_planes[g // PLANES_PER_TILE][offset:P, lo : lo + wid],
                start=(g == 0),
                stop=(g == PASSES - 1),
            )

        for u in range(N_BANKS):
            open_unit()
        late_from = {}
        for b, (width, runs) in enumerate(BLOCKS):
            for u in blocks[b]:
                late_from[u] = runs[0][0]
        for g in range(WIDE_PASSES):
            for u in range(N_BANKS):
                if g < late_from[u]:
                    mx_pass(g, u)

        first = 0
        for b, width in enumerate(BLOCK_WIDTHS):
            for g in range(BLOCKS[b][1][0][0], PASSES):
                for u in blocks[b]:
                    mx_pass(g, u)
            y = keep.tile([P, width], F32, name="y%d" % b)
            pieces = []
            for u in blocks[b]:
                lo, wid = units[u]
                cut = wid if len(blocks[b]) > 1 else wid // 2
                for off in range(0, wid, cut):
                    pieces.append((u, off, lo - first + off, cut))
            for u, off, lo, cut in pieces:
                nc.vector.tensor_mul(
                    out=y[:, lo : lo + cut],
                    in0=accs[u][:, off : off + cut],
                    in1=gain_all[:, first + lo : first + lo + cut],
                )
            for u, off, lo, cut in pieces:
                nc.vector.tensor_add(
                    out=y[:, lo : lo + cut],
                    in0=y[:, lo : lo + cut],
                    in1=shift_all[:, first + lo : first + lo + cut],
                )
            for u, off, lo, cut in pieces:
                nc.vector.tensor_scalar_max(out=y[:, lo : lo + cut], in0=y[:, lo : lo + cut], scalar1=0.0)
            for u, off, lo, cut in pieces:
                nc.scalar.activation(
                    out=y[:, lo : lo + cut], in_=y[:, lo : lo + cut], func=ACT.Gelu_apprx_tanh
                )
            queue = nc.scalar if b >= len(BLOCK_WIDTHS) - 2 else nc.sync
            queue.dma_start(out=out[:, first : first + width], in_=y[:])
            first += width
            if b == 0:
                for u in range(N_BANKS, len(units)):
                    open_unit()
                for g in range(WIDE_PASSES):
                    for u in range(N_BANKS, len(units)):
                        if g < late_from[u]:
                            mx_pass(g, u)
